import numpy as np
import ml_dtypes


def mxq(x, axis, fmt="e4m3"):
    dtype, down = {"e4m3": (ml_dtypes.float8_e4m3fn, 7), "e5m2": (ml_dtypes.float8_e5m2, 14)}[fmt]
    v = np.moveaxis(np.asarray(x, np.float32).astype(ml_dtypes.bfloat16).astype(np.float64), axis, -1)
    blocks = v.reshape(v.shape[:-1] + (-1, 32))
    amax = np.abs(blocks).max(-1, keepdims=True)
    byte = np.maximum(np.where(amax > 0, np.frexp(amax)[1] - 1 + 127, 0) - down, 1)
    scale = np.exp2(byte - 127.0)
    codes = (blocks / scale).astype(np.float32).astype(dtype).astype(np.float64)
    return np.moveaxis((codes * scale).reshape(v.shape), -1, axis)


WIDE = False


def mx_kscale(k):
    if not WIDE:
        return np.ones(k)
    levels = np.array([10, -10, 5, -5, 0])
    if k % 512:
        return np.exp2(np.random.permutation(np.resize(levels, k // 32))).repeat(32)
    a = np.empty((k // 512, 16))
    for p in range(k // 512):
        a[p, :8] = np.random.permutation(np.resize(levels, 8))
        for g in range(8):
            far = levels[np.abs(levels - a[p, g]) >= 10]
            a[p, g + 8] = far[np.random.randint(len(far))]
    return np.exp2(a.ravel()).repeat(32)


BF16 = ml_dtypes.bfloat16


def bf(x):
    return np.asarray(x, np.float32).astype(BF16)


def f64(x):
    return np.asarray(x).astype(np.float64)


B, S, W, QK, E, V, H = 1, 1024, 1024, 128, 2048, 1024, 1
N = 2 * QK + 2 * E


def erf(v):
    a = np.clip(v, -6.0, 6.0)
    a2 = a * a
    term = a.copy()
    tot = a.copy()
    for n in range(1, 100):
        term = term * (a2 / (n + 0.5))
        tot = tot + term
    return 2.0 / np.sqrt(np.pi) * np.exp(-a2) * tot


def gelu_erf(v):
    return 0.5 * v * (1.0 + erf(v / np.sqrt(2.0)))


def setup_inputs():
    s = mx_kscale(W)
    g = np.where(np.arange(N) < 2 * QK, 1.4, 1.0)
    return {"x": bf(np.random.standard_normal((B, S, W)) * 1.5 + 0.5),
            "norm_w": bf((1.0 + 0.1 * np.random.standard_normal(W)) * s),
            "expand_w": bf(np.random.standard_normal((N, W)) * g[:, None] / np.sqrt(W) / s[None, :])}


def reference(x, norm_w, expand_w):
    x = f64(x)
    mu = x.mean(-1, keepdims=True)
    var = x.var(-1, keepdims=True)
    xn = (x - mu) / np.sqrt(var + 1e-5) * f64(norm_w)
    hidden = mxq(xn, 2, "e4m3") @ mxq(f64(expand_w), 1, "e4m3").T
    q = hidden[..., :QK]
    k = hidden[..., QK:2 * QK]
    lin = hidden[..., 2 * QK:2 * QK + E]
    pre = hidden[..., 2 * QK + E:]
    geglu = lin * gelu_erf(pre)
    return q, k, geglu

@@ -1,0 +1,277 @@
+from contextlib import ExitStack
+
+import concourse.masks as masks
+import concourse.mybir as mybir
+
+F32 = mybir.dt.float32
+BF16 = mybir.dt.bfloat16
+U32 = mybir.dt.uint32
+U8 = mybir.dt.uint8
+FP8X4 = mybir.dt.float8_e4m3fn_x4
+ACT = mybir.ActivationFunctionType
+ALU = mybir.AluOpType
+
+P = 128
+PACK = 4
+K = 1024
+PASSES = K // (P * PACK)
+WORDS = K // 2
+ROWS = 1024
+N_BLOCKS = ROWS // P
+HEAD = 128
+QK = 2 * HEAD
+E = 2048
+CHUNK = 512
+N_PAIRS = E // CHUNK
+PRE, LIN = 0, 1
+QK_CHUNK = 2 * N_PAIRS
+RUN_ROW_BLOCKS = 2
+N_RUNS = 2 * QK_CHUNK + 1
+BN_STATS_MAX = 512
+EPS = 1e-5
+N_BANKS = 8
+
+FIRST_BLOCKS = 4
+STEPS = 4
+N_PRODUCTS = N_BLOCKS * N_PAIRS
+RUNS_AHEAD = 4
+STATISTICS_AHEAD = 8
+TRANSPOSE_AHEAD = 3
+QUANTISE_AHEAD = 2
+
+FLOPS = 2 * ROWS * K * (QK + 2 * E)
+
+
+def tile_latentattentionblock_pa_kernel(tc, x, norm_w, expand_w, out_0, out_1, out_2):
+    nc = tc.nc
+    with ExitStack() as ctx:
+        ctx.enter_context(tc.manual_schedule())
+        resident = ctx.enter_context(tc.tile_pool(name="resident", bufs=1))
+        per_block = ctx.enter_context(tc.tile_pool(name="per_block", bufs=FIRST_BLOCKS))
+        grouped_tiles = ctx.enter_context(tc.tile_pool(name="grouped_tiles", bufs=2))
+        gates = ctx.enter_context(tc.tile_pool(name="gates", bufs=N_BANKS // 2 + 1))
+        results = ctx.enter_context(tc.tile_pool(name="results", bufs=12))
+        banks = ctx.enter_context(tc.psum_pool(name="banks", bufs=N_BANKS))
+
+        x_rows = x.rearrange("o (p i) w -> p (o i) w", i=N_BLOCKS)
+        q_rows = out_0.rearrange("o (p i) d -> p (o i) d", i=N_BLOCKS)
+        k_rows = out_1.rearrange("o (p i) d -> p (o i) d", i=N_BLOCKS)
+        geglu_rows = out_2.rearrange("o (p i) d -> p (o i) d", i=N_BLOCKS)
+
+        x_raw = resident.tile([P, N_BLOCKS, K], BF16, name="x_raw")
+        w_raw = resident.tile([P, (QK + 2 * E) // P * K], BF16, name="w_raw")
+        w_words = w_raw[:].bitcast(F32)
+        x_codes = resident.tile([P, N_BLOCKS * PASSES * P], U32, name="x_codes", align_bytes=64)
+        x_scales = resident.tile([P, N_BLOCKS * PASSES * P], U8, name="x_scales", align_bytes=64)
+        w_codes = resident.tile([P, PASSES * (2 * E + QK)], U32, name="w_codes", align_bytes=64)
+        w_scales = resident.tile([P, PASSES * (2 * E + QK)], U8, name="w_scales", align_bytes=64)
+        qk_stage = resident.tile([P, 2, N_BLOCKS, HEAD], F32, name="qk_stage")
+        identity = resident.tile([P, P], F32, name="identity")
+        gain_rows = resident.tile([P, PACK * P], BF16, name="gain_rows")
+        gain = resident.tile([P, PASSES * PACK], F32, name="gain")
+        minus_half = resident.tile([P, 1], F32, name="minus_half")
+        warm = resident.tile([P, 1], F32, name="warm")
+
+        def load_x(first, count):
+            blocks = slice(first, first + count)
+            nc.sync.dma_start(out=x_raw[:, blocks, :], in_=x_rows[:, blocks, :])
+
+        def chunk_width(chunk):
+            return QK if chunk == QK_CHUNK else CHUNK
+
+        def chunk_row_block(chunk):
+            if chunk == QK_CHUNK:
+                return 0
+            lin_first = (QK + chunk // 2 * CHUNK) // P
+            return lin_first if chunk % 2 == LIN else lin_first + E // P
+
+        def load_chunk(chunk, pieces):
+            count = chunk_width(chunk) // P // pieces
+            for piece in range(pieces):
+                first = chunk_row_block(chunk) + piece * count
+                nc.sync.dma_start(
+                    out=w_raw[:, first * K : (first + count) * K].rearrange("p (i k) -> p i k", k=K),
+                    in_=expand_w[first * P : (first + count) * P, :].rearrange("(i p) k -> p i k", p=P),
+                )
+
+        normalised = {}
+        x_grouped = {}
+
+        def x_normalise(b):
+            stats = per_block.tile([P, K // BN_STATS_MAX, 6], F32, name="stats", tag="stats")
+            for h in range(K // BN_STATS_MAX):
+                nc.vector.bn_stats(out=stats[:, h, :], in_=x_raw[:, b, h * BN_STATS_MAX : (h + 1) * BN_STATS_MAX])
+            moments = per_block.tile([P, 3], F32, name="moments", tag="moments")
+            nc.vector.bn_aggr(out=moments[:, 0:2], in_=stats[:].rearrange("p h c -> p (h c)"))
+            nc.vector.tensor_scalar_add(out=moments[:, 2:3], in0=moments[:, 1:2], scalar1=EPS)
+            scale_bias = per_block.tile([P, 2], F32, name="scale_bias", tag="scale_bias")
+            nc.gpsimd.tensor_tensor(out=scale_bias[:, 0:1], in0=moments[:, 2:3], in1=minus_half[:], op=ALU.pow)
+            nc.gpsimd.tensor_scalar(
+                out=scale_bias[:, 1:2],
+                in0=moments[:, 0:1],
+                scalar1=scale_bias[:, 0:1],
+                scalar2=-1.0,
+                op0=ALU.mult,
+                op1=ALU.mult,
+            )
+            y = per_block.tile([P, K], F32, name="y", tag="y")
+            nc.gpsimd.tensor_scalar(
+                out=y[:].rearrange("p (g t q) -> p g t q", t=PACK, q=P),
+                in0=x_raw[:, b, :].rearrange("p (g q t) -> p g t q", t=PACK, q=P),
+                scalar1=scale_bias[:, 0:1],
+                scalar2=scale_bias[:, 1:2],
+                op0=ALU.mult,
+                op1=ALU.add,
+            )
+            normalised[b] = y
+
+        def spread_gain():
+            gain_bank = banks.tile([P, 2 * P], F32, name="gain_bank", tag="bank")
+            for u in range(2):
+                nc.tensor.transpose(
+                    gain_bank[:, u * P : (u + 1) * P], gain_rows[:].bitcast(F32)[:, u : 2 * P : 2], identity[:]
+                )
+            nc.vector.tensor_copy(
+                out=gain[:].rearrange("p (g u e) -> p g u e", u=2, e=2),
+                in_=gain_bank[:].bitcast(BF16).rearrange("p (u r e) -> p r u e", u=2, e=2)[:, 0:PASSES, :, :],
+            )
+
+        def x_transpose(b):
+            y = normalised[b]
+            grouped = grouped_tiles.tile([P, PASSES * P * PACK], BF16, name="x_grouped", tag="x", align_bytes=64)
+            for g in range(PASSES):
+                bank = banks.tile([P, PACK * P], F32, name="x_bank", tag="bank")
+                for t in range(PACK):
+                    column = (g * PACK + t) * P
+                    nc.tensor.transpose(bank[:, t * P : (t + 1) * P], y[:, column : column + P], identity[:])
+                nc.vector.tensor_tensor(
+                    out=grouped[:, g * P * PACK : (g + 1) * P * PACK].rearrange("p (r t) -> p r t", t=PACK),
+                    in0=bank[:].rearrange("p (t r) -> p r t", t=PACK),
+                    in1=gain[:, g * PACK : (g + 1) * PACK].unsqueeze(1).to_broadcast([P, P, PACK]),
+                    op=ALU.mult,
+                )
+            x_grouped[b] = grouped
+
+        def x_quantise(b):
+            columns = slice(b * PASSES * P, (b + 1) * PASSES * P)
+            nc.vector.quantize_mx(
+                out=x_codes[:, columns].bitcast(FP8X4), scales=x_scales[:, columns], in_=x_grouped[b][:]
+            )
+
+        w_grouped = {}
+
+        def w_transpose(run):
+            chunk = run // 2
+            if run % 2 == 0:
+                w_grouped[chunk] = grouped_tiles.tile(
+                    [P, PASSES * chunk_width(chunk) * PACK], BF16, name="w_grouped", tag="w", align_bytes=64
+                )
+            grouped_words = w_grouped[chunk][:].bitcast(F32).rearrange("p (g n u) -> p g n u", g=PASSES, u=2)
+            for i in range(RUN_ROW_BLOCKS):
+                block = run % 2 * RUN_ROW_BLOCKS + i
+                bank = banks.tile([P, PACK * P], F32, name="w_bank", tag="bank")
+                for a in range(PACK):
+                    first = (chunk_row_block(chunk) + block) * WORDS + a // 2 * 2 * P
+                    nc.tensor.transpose(
+                        bank[:, a * P : (a + 1) * P], w_words[:, first + a % 2 : first + 2 * P : 2], identity[:]
+                    )
+                nc.scalar.copy(
+                    out=grouped_words[:, :, block * P : (block + 1) * P, :],
+                    in_=bank[:].rearrange("p (g u r) -> p g r u", g=PASSES, u=2),
+                )
+
+        def completes_chunk(run):
+            return 0 <= run < N_RUNS and (run % 2 == 1 or run // 2 == QK_CHUNK)
+
+        def w_quantise(chunk):
+            first = chunk * PASSES * CHUNK
+            columns = slice(first, first + PASSES * chunk_width(chunk))
+            nc.vector.quantize_mx(
+                out=w_codes[:, columns].bitcast(FP8X4), scales=w_scales[:, columns], in_=w_grouped[chunk][:]
+            )
+
+        def multiply(acc, b, chunk):
+            width = chunk_width(chunk)
+            for g in range(PASSES):
+                rows = slice((b * PASSES + g) * P, (b * PASSES + g + 1) * P)
+                first = chunk * PASSES * CHUNK + g * width
+                columns = slice(first, first + width)
+                nc.tensor.matmul_mx(
+                    out=acc,
+                    lhsT=x_codes[:, rows].bitcast(FP8X4),
+                    lhsT_scale=x_scales[:, rows],
+                    rhs=w_codes[:, columns].bitcast(FP8X4),
+                    rhs_scale=w_scales[:, columns],
+                    start=(g == 0),
+                    stop=(g == PASSES - 1),
+                )
+
+        def project_qk(b):
+            acc = banks.tile([P, QK], F32, name="qk_acc", tag="bank")
+            multiply(acc[:], b, QK_CHUNK)
+            nc.scalar.copy(out=qk_stage[:, :, b, :], in_=acc[:].rearrange("p (h d) -> p h d", h=2))
+
+        def multiply_pair(b, pair):
+            pre = banks.tile([P, CHUNK], F32, name="pre", tag="bank")
+            multiply(pre[:], b, 2 * pair + PRE)
+            lin = banks.tile([P, CHUNK], F32, name="lin", tag="bank")
+            multiply(lin[:], b, 2 * pair + LIN)
+            gate = gates.tile([P, CHUNK], F32, name="gate", tag="gate")
+            nc.scalar.activation(out=gate[:], in_=pre[:], func=ACT.Gelu)
+            return b, pair, lin, gate
+
+        def gate_and_store(product):
+            b, pair, lin, gate = product
+            geglu = results.tile([P, CHUNK], F32, name="geglu", tag="geglu")
+            nc.vector.tensor_tensor(out=geglu[:], in0=lin[:], in1=gate[:], op=ALU.mult)
+            nc.sync.dma_start(out=geglu_rows[:, b, pair * CHUNK : (pair + 1) * CHUNK], in_=geglu[:])
+
+        nc.vector.memset(gain_rows[:].bitcast(F32), 0.0)
+        nc.vector.memset(minus_half[:], -0.5)
+        nc.scalar.activation(out=warm[:], in_=minus_half[:], func=ACT.Gelu)
+        masks.make_identity(nc, identity[:])
+
+        load_x(0, 1)
+        nc.sync.dma_start(out=gain_rows[0:PASSES, :], in_=norm_w.rearrange("(g c) -> g c", g=PASSES))
+        for b in range(1, FIRST_BLOCKS):
+            load_x(b, 1)
+        for chunk in range(QK_CHUNK + 1):
+            load_chunk(chunk, 2 if chunk // 2 == 0 else 1)
+            if chunk == 2 * 1 + LIN:
+                load_x(FIRST_BLOCKS, N_BLOCKS - FIRST_BLOCKS)
+
+        def block_starting_at(n):
+            if 0 <= n < FIRST_BLOCKS:
+                return n
+            if n % STEPS == 0 and FIRST_BLOCKS <= n // STEPS < N_BLOCKS:
+                return n // STEPS
+            return None
+
+        product_waiting = None
+        for n in range(-STATISTICS_AHEAD, N_PRODUCTS):
+            rnd, step = n // STEPS, n % STEPS
+            run = n + RUNS_AHEAD
+            if completes_chunk(run - 1):
+                w_quantise((run - 1) // 2)
+            if product_waiting is not None:
+                gate_and_store(product_waiting)
+            if block_starting_at(n + STATISTICS_AHEAD) is not None:
+                x_normalise(block_starting_at(n + STATISTICS_AHEAD))
+            if step == 0 and rnd >= FIRST_BLOCKS:
+                project_qk(rnd - FIRST_BLOCKS)
+                project_qk(rnd)
+            if n == N_PRODUCTS - STEPS:
+                nc.sync.dma_start(out=q_rows, in_=qk_stage[:, 0, :, :])
+                nc.sync.dma_start(out=k_rows, in_=qk_stage[:, 1, :, :])
+            if 0 <= run < N_RUNS:
+                w_transpose(run)
+            if n + TRANSPOSE_AHEAD == 0:
+                spread_gain()
+            if block_starting_at(n + TRANSPOSE_AHEAD) is not None:
+                x_transpose(block_starting_at(n + TRANSPOSE_AHEAD))
+            if block_starting_at(n + QUANTISE_AHEAD) is not None:
+                x_quantise(block_starting_at(n + QUANTISE_AHEAD))
+            if n >= 0:
+                b, pair = (step, rnd) if rnd < FIRST_BLOCKS else (rnd, step)
+                product_waiting = multiply_pair(b, pair)
+        gate_and_store(product_waiting)

@@ -37,6 +37,7 @@ N_PRODUCTS = N_BLOCKS * N_PAIRS
 RUNS_AHEAD = 4
 STATISTICS_AHEAD = 8
 TRANSPOSE_AHEAD = 3
+QK_FROM = 18
 QUANTISE_AHEAD = 2
 
 FLOPS = 2 * ROWS * K * (QK + 2 * E)
@@ -211,17 +212,21 @@ def tile_latentattentionblock_pa_kernel(tc, x, norm_w, expand_w, out_0, out_1, o
             multiply(acc[:], b, QK_CHUNK)
             nc.scalar.copy(out=qk_stage[:, :, b, :], in_=acc[:].rearrange("p (h d) -> p h d", h=2))
 
-        def multiply_pair(b, pair):
+        def multiply_pre(b, pair):
             pre = banks.tile([P, CHUNK], F32, name="pre", tag="bank")
             multiply(pre[:], b, 2 * pair + PRE)
-            lin = banks.tile([P, CHUNK], F32, name="lin", tag="bank")
-            multiply(lin[:], b, 2 * pair + LIN)
             gate = gates.tile([P, CHUNK], F32, name="gate", tag="gate")
             nc.scalar.activation(out=gate[:], in_=pre[:], func=ACT.Gelu)
-            return b, pair, lin, gate
+            return b, pair, gate
+
+        def multiply_lin(product):
+            b, pair, gate = product
+            lin = banks.tile([P, CHUNK], F32, name="lin", tag="bank")
+            multiply(lin[:], b, 2 * pair + LIN)
+            return b, pair, gate, lin
 
         def gate_and_store(product):
-            b, pair, lin, gate = product
+            b, pair, gate, lin = product
             geglu = results.tile([P, CHUNK], F32, name="geglu", tag="geglu")
             nc.vector.tensor_tensor(out=geglu[:], in0=lin[:], in1=gate[:], op=ALU.mult)
             nc.sync.dma_start(out=geglu_rows[:, b, pair * CHUNK : (pair + 1) * CHUNK], in_=geglu[:])
@@ -240,38 +245,39 @@ def tile_latentattentionblock_pa_kernel(tc, x, norm_w, expand_w, out_0, out_1, o
             if chunk == 2 * 1 + LIN:
                 load_x(FIRST_BLOCKS, N_BLOCKS - FIRST_BLOCKS)
 
-        def block_starting_at(n):
+        def block_due_at(n):
             if 0 <= n < FIRST_BLOCKS:
                 return n
-            if n % STEPS == 0 and FIRST_BLOCKS <= n // STEPS < N_BLOCKS:
-                return n // STEPS
+            late = n - FIRST_BLOCKS * STEPS
+            if late >= 0 and late % 3 == 0 and late // 3 < N_BLOCKS - FIRST_BLOCKS:
+                return FIRST_BLOCKS + late // 3
             return None
 
-        product_waiting = None
-        for n in range(-STATISTICS_AHEAD, N_PRODUCTS):
+        held = None
+        for n in range(-STATISTICS_AHEAD, N_PRODUCTS + 1):
             rnd, step = n // STEPS, n % STEPS
             run = n + RUNS_AHEAD
             if completes_chunk(run - 1):
                 w_quantise((run - 1) // 2)
-            if product_waiting is not None:
-                gate_and_store(product_waiting)
-            if block_starting_at(n + STATISTICS_AHEAD) is not None:
-                x_normalise(block_starting_at(n + STATISTICS_AHEAD))
-            if step == 0 and rnd >= FIRST_BLOCKS:
-                project_qk(rnd - FIRST_BLOCKS)
-                project_qk(rnd)
-            if n == N_PRODUCTS - STEPS:
+            if block_due_at(n + STATISTICS_AHEAD) is not None:
+                x_normalise(block_due_at(n + STATISTICS_AHEAD))
+            if 0 <= n - QK_FROM < N_BLOCKS:
+                project_qk(n - QK_FROM)
+            if n == QK_FROM + N_BLOCKS:
                 nc.sync.dma_start(out=q_rows, in_=qk_stage[:, 0, :, :])
                 nc.sync.dma_start(out=k_rows, in_=qk_stage[:, 1, :, :])
             if 0 <= run < N_RUNS:
                 w_transpose(run)
             if n + TRANSPOSE_AHEAD == 0:
                 spread_gain()
-            if block_starting_at(n + TRANSPOSE_AHEAD) is not None:
-                x_transpose(block_starting_at(n + TRANSPOSE_AHEAD))
-            if block_starting_at(n + QUANTISE_AHEAD) is not None:
-                x_quantise(block_starting_at(n + QUANTISE_AHEAD))
-            if n >= 0:
+            if block_due_at(n + TRANSPOSE_AHEAD) is not None:
+                x_transpose(block_due_at(n + TRANSPOSE_AHEAD))
+            if block_due_at(n + QUANTISE_AHEAD) is not None:
+                x_quantise(block_due_at(n + QUANTISE_AHEAD))
+            product = None if held is None else multiply_lin(held)
+            held = None
+            if 0 <= n < N_PRODUCTS:
                 b, pair = (step, rnd) if rnd < FIRST_BLOCKS else (rnd, step)
-                product_waiting = multiply_pair(b, pair)
-        gate_and_store(product_waiting)
+                held = multiply_pre(b, pair)
+            if product is not None:
+                gate_and_store(product)

@@ -38,6 +38,8 @@ RUNS_AHEAD = 4
 STATISTICS_AHEAD = 8
 TRANSPOSE_AHEAD = 3
 QK_FROM = 18
+LATE_AHEAD = 11
+APPLY_AHEAD = 7
 QUANTISE_AHEAD = 2
 
 FLOPS = 2 * ROWS * K * (QK + 2 * E)
@@ -71,6 +73,7 @@ def tile_latentattentionblock_pa_kernel(tc, x, norm_w, expand_w, out_0, out_1, o
         gain_rows = resident.tile([P, PACK * P], BF16, name="gain_rows")
         gain = resident.tile([P, PASSES * PACK], F32, name="gain")
         minus_half = resident.tile([P, 1], F32, name="minus_half")
+        filler = resident.tile([P, CHUNK], BF16, name="filler")
         warm = resident.tile([P, 1], F32, name="warm")
 
         def load_x(first, count):
@@ -98,32 +101,40 @@ def tile_latentattentionblock_pa_kernel(tc, x, norm_w, expand_w, out_0, out_1, o
         normalised = {}
         x_grouped = {}
 
-        def x_normalise(b):
+        statistics = {}
+        moments_of = {}
+        scale_of = {}
+
+        def x_statistics(b):
             stats = per_block.tile([P, K // BN_STATS_MAX, 6], F32, name="stats", tag="stats")
             for h in range(K // BN_STATS_MAX):
                 nc.vector.bn_stats(out=stats[:, h, :], in_=x_raw[:, b, h * BN_STATS_MAX : (h + 1) * BN_STATS_MAX])
-            moments = per_block.tile([P, 3], F32, name="moments", tag="moments")
-            nc.vector.bn_aggr(out=moments[:, 0:2], in_=stats[:].rearrange("p h c -> p (h c)"))
+            statistics[b] = stats
+
+        def x_scale(b):
+            moments = per_block.tile([P, 4], F32, name="moments", tag="moments")
+            nc.vector.bn_aggr(out=moments[:, 0:2], in_=statistics[b][:].rearrange("p h c -> p (h c)"))
             nc.vector.tensor_scalar_add(out=moments[:, 2:3], in0=moments[:, 1:2], scalar1=EPS)
-            scale_bias = per_block.tile([P, 2], F32, name="scale_bias", tag="scale_bias")
-            nc.gpsimd.tensor_tensor(out=scale_bias[:, 0:1], in0=moments[:, 2:3], in1=minus_half[:], op=ALU.pow)
-            nc.gpsimd.tensor_scalar(
-                out=scale_bias[:, 1:2],
-                in0=moments[:, 0:1],
-                scalar1=scale_bias[:, 0:1],
-                scalar2=-1.0,
-                op0=ALU.mult,
-                op1=ALU.mult,
-            )
+            nc.vector.tensor_scalar_mul(out=moments[:, 3:4], in0=moments[:, 0:1], scalar1=-1.0)
+            scale = per_block.tile([P, 2], F32, name="scale", tag="scale")
+            nc.gpsimd.tensor_tensor(out=scale[:, 0:1], in0=moments[:, 2:3], in1=minus_half[:], op=ALU.pow)
+            moments_of[b] = moments
+            scale_of[b] = scale
+
+        def x_normalise(b):
+            minus_mean, scale = moments_of[b][:, 3:4], scale_of[b]
             y = per_block.tile([P, K], F32, name="y", tag="y")
-            nc.gpsimd.tensor_scalar(
-                out=y[:].rearrange("p (g t q) -> p g t q", t=PACK, q=P),
-                in0=x_raw[:, b, :].rearrange("p (g q t) -> p g t q", t=PACK, q=P),
-                scalar1=scale_bias[:, 0:1],
-                scalar2=scale_bias[:, 1:2],
-                op0=ALU.mult,
-                op1=ALU.add,
-            )
+            parted = y[:].rearrange("p (g t q) -> p g t q", t=PACK, q=P)
+            features = x_raw[:, b, :].rearrange("p (g q t) -> p g t q", t=PACK, q=P)
+            if b < FIRST_BLOCKS:
+                nc.gpsimd.tensor_scalar(
+                    out=parted, in0=features, scalar1=minus_mean, scalar2=scale[:, 0:1], op0=ALU.add, op1=ALU.mult
+                )
+            else:
+                nc.scalar.activation(out=scale[:, 1:2], in_=minus_mean, func=ACT.Copy, scale=scale[:, 0:1])
+                nc.scalar.activation(
+                    out=parted, in_=features, func=ACT.Identity, scale=scale[:, 0:1], bias=scale[:, 1:2]
+                )
             normalised[b] = y
 
         def spread_gain():
@@ -231,8 +242,14 @@ def tile_latentattentionblock_pa_kernel(tc, x, norm_w, expand_w, out_0, out_1, o
             nc.vector.tensor_tensor(out=geglu[:], in0=lin[:], in1=gate[:], op=ALU.mult)
             nc.sync.dma_start(out=geglu_rows[:, b, pair * CHUNK : (pair + 1) * CHUNK], in_=geglu[:])
 
+        def keep_busy(count):
+            idle_bank = banks.tile([P, CHUNK], F32, name="idle_bank", tag="bank")
+            for i in range(count):
+                nc.tensor.matmul(idle_bank[:], lhsT=filler[:, 0:P], rhs=filler[:], start=True, stop=True)
+
         nc.vector.memset(gain_rows[:].bitcast(F32), 0.0)
         nc.vector.memset(minus_half[:], -0.5)
+        nc.vector.memset(filler[:], 1.0)
         nc.scalar.activation(out=warm[:], in_=minus_half[:], func=ACT.Gelu)
         masks.make_identity(nc, identity[:])
 
@@ -253,14 +270,17 @@ def tile_latentattentionblock_pa_kernel(tc, x, norm_w, expand_w, out_0, out_1, o
                 return FIRST_BLOCKS + late // 3
             return None
 
+        keep_busy(8)
         held = None
         for n in range(-STATISTICS_AHEAD, N_PRODUCTS + 1):
             rnd, step = n // STEPS, n % STEPS
             run = n + RUNS_AHEAD
             if completes_chunk(run - 1):
                 w_quantise((run - 1) // 2)
-            if block_due_at(n + STATISTICS_AHEAD) is not None:
-                x_normalise(block_due_at(n + STATISTICS_AHEAD))
+            if 0 <= n + STATISTICS_AHEAD < FIRST_BLOCKS:
+                x_statistics(n + STATISTICS_AHEAD)
+                x_scale(n + STATISTICS_AHEAD)
+                x_normalise(n + STATISTICS_AHEAD)
             if 0 <= n - QK_FROM < N_BLOCKS:
                 project_qk(n - QK_FROM)
             if n == QK_FROM + N_BLOCKS:
@@ -279,5 +299,14 @@ def tile_latentattentionblock_pa_kernel(tc, x, norm_w, expand_w, out_0, out_1, o
             if 0 <= n < N_PRODUCTS:
                 b, pair = (step, rnd) if rnd < FIRST_BLOCKS else (rnd, step)
                 held = multiply_pre(b, pair)
+            ready = block_due_at(n + APPLY_AHEAD)
+            if ready is not None and ready >= FIRST_BLOCKS:
+                x_normalise(ready)
+            begun = block_due_at(n + LATE_AHEAD)
+            begun = None if begun is None or begun < FIRST_BLOCKS else begun
+            if begun is not None:
+                x_statistics(begun)
             if product is not None:
                 gate_and_store(product)
+            if begun is not None:
+                x_scale(begun)

from contextlib import ExitStack

import concourse.masks as masks
import concourse.mybir as mybir

F32 = mybir.dt.float32
BF16 = mybir.dt.bfloat16
U32 = mybir.dt.uint32
U8 = mybir.dt.uint8
FP8X4 = mybir.dt.float8_e4m3fn_x4
ACT = mybir.ActivationFunctionType
ALU = mybir.AluOpType

P = 128
PACK = 4
K = 1024
PASSES = K // (P * PACK)
WORDS = K // 2
ROWS = 1024
N_BLOCKS = ROWS // P
HEAD = 128
QK = 2 * HEAD
E = 2048
CHUNK = 512
N_PAIRS = E // CHUNK
PRE, LIN = 0, 1
QK_CHUNK = 2 * N_PAIRS
RUN_ROW_BLOCKS = 2
N_RUNS = 2 * QK_CHUNK + 1
BN_STATS_MAX = 512
EPS = 1e-5
N_BANKS = 8

FIRST_BLOCKS = 4
STEPS = 4
N_PRODUCTS = N_BLOCKS * N_PAIRS
RUNS_AHEAD = 4
STATISTICS_AHEAD = 8
TRANSPOSE_AHEAD = 3
QK_FROM = 18
LATE_AHEAD = 11
APPLY_AHEAD = 7
QUANTISE_AHEAD = 2

FLOPS = 2 * ROWS * K * (QK + 2 * E)


def tile_latentattentionblock_pa_kernel(tc, x, norm_w, expand_w, out_0, out_1, out_2):
    nc = tc.nc
    with ExitStack() as ctx:
        ctx.enter_context(tc.manual_schedule())
        resident = ctx.enter_context(tc.tile_pool(name="resident", bufs=1))
        per_block = ctx.enter_context(tc.tile_pool(name="per_block", bufs=FIRST_BLOCKS))
        grouped_tiles = ctx.enter_context(tc.tile_pool(name="grouped_tiles", bufs=2))
        gates = ctx.enter_context(tc.tile_pool(name="gates", bufs=N_BANKS // 2 + 1))
        results = ctx.enter_context(tc.tile_pool(name="results", bufs=12))
        banks = ctx.enter_context(tc.psum_pool(name="banks", bufs=N_BANKS))

        x_rows = x.rearrange("o (p i) w -> p (o i) w", i=N_BLOCKS)
        q_rows = out_0.rearrange("o (p i) d -> p (o i) d", i=N_BLOCKS)
        k_rows = out_1.rearrange("o (p i) d -> p (o i) d", i=N_BLOCKS)
        geglu_rows = out_2.rearrange("o (p i) d -> p (o i) d", i=N_BLOCKS)

        x_raw = resident.tile([P, N_BLOCKS, K], BF16, name="x_raw")
        w_raw = resident.tile([P, (QK + 2 * E) // P * K], BF16, name="w_raw")
        w_words = w_raw[:].bitcast(F32)
        x_codes = resident.tile([P, N_BLOCKS * PASSES * P], U32, name="x_codes", align_bytes=64)
        x_scales = resident.tile([P, N_BLOCKS * PASSES * P], U8, name="x_scales", align_bytes=64)
        w_codes = resident.tile([P, PASSES * (2 * E + QK)], U32, name="w_codes", align_bytes=64)
        w_scales = resident.tile([P, PASSES * (2 * E + QK)], U8, name="w_scales", align_bytes=64)
        qk_stage = resident.tile([P, 2, N_BLOCKS, HEAD], F32, name="qk_stage")
        identity = resident.tile([P, P], F32, name="identity")
        gain_rows = resident.tile([P, PACK * P], BF16, name="gain_rows")
        gain = resident.tile([P, PASSES * PACK], F32, name="gain")
        minus_half = resident.tile([P, 1], F32, name="minus_half")
        filler = resident.tile([P, CHUNK], BF16, name="filler")
        warm = resident.tile([P, 1], F32, name="warm")

        def load_x(first, count):
            blocks = slice(first, first + count)
            nc.sync.dma_start(out=x_raw[:, blocks, :], in_=x_rows[:, blocks, :])

        def chunk_width(chunk):
            return QK if chunk == QK_CHUNK else CHUNK

        def chunk_row_block(chunk):
            if chunk == QK_CHUNK:
                return 0
            lin_first = (QK + chunk // 2 * CHUNK) // P
            return lin_first if chunk % 2 == LIN else lin_first + E // P

        def load_chunk(chunk, pieces):
            count = chunk_width(chunk) // P // pieces
            for piece in range(pieces):
                first = chunk_row_block(chunk) + piece * count
                nc.sync.dma_start(
                    out=w_raw[:, first * K : (first + count) * K].rearrange("p (i k) -> p i k", k=K),
                    in_=expand_w[first * P : (first + count) * P, :].rearrange("(i p) k -> p i k", p=P),
                )

        normalised = {}
        x_grouped = {}

        statistics = {}
        moments_of = {}
        scale_of = {}

        def x_statistics(b):
            stats = per_block.tile([P, K // BN_STATS_MAX, 6], F32, name="stats", tag="stats")
            for h in range(K // BN_STATS_MAX):
                nc.vector.bn_stats(out=stats[:, h, :], in_=x_raw[:, b, h * BN_STATS_MAX : (h + 1) * BN_STATS_MAX])
            statistics[b] = stats

        def x_scale(b):
            moments = per_block.tile([P, 4], F32, name="moments", tag="moments")
            nc.vector.bn_aggr(out=moments[:, 0:2], in_=statistics[b][:].rearrange("p h c -> p (h c)"))
            nc.vector.tensor_scalar_add(out=moments[:, 2:3], in0=moments[:, 1:2], scalar1=EPS)
            nc.vector.tensor_scalar_mul(out=moments[:, 3:4], in0=moments[:, 0:1], scalar1=-1.0)
            scale = per_block.tile([P, 2], F32, name="scale", tag="scale")
            nc.gpsimd.tensor_tensor(out=scale[:, 0:1], in0=moments[:, 2:3], in1=minus_half[:], op=ALU.pow)
            moments_of[b] = moments
            scale_of[b] = scale

        def x_normalise(b):
            minus_mean, scale = moments_of[b][:, 3:4], scale_of[b]
            y = per_block.tile([P, K], F32, name="y", tag="y")
            parted = y[:].rearrange("p (g t q) -> p g t q", t=PACK, q=P)
            features = x_raw[:, b, :].rearrange("p (g q t) -> p g t q", t=PACK, q=P)
            if b < FIRST_BLOCKS:
                nc.gpsimd.tensor_scalar(
                    out=parted, in0=features, scalar1=minus_mean, scalar2=scale[:, 0:1], op0=ALU.add, op1=ALU.mult
                )
            else:
                nc.scalar.activation(out=scale[:, 1:2], in_=minus_mean, func=ACT.Copy, scale=scale[:, 0:1])
                nc.scalar.activation(
                    out=parted, in_=features, func=ACT.Identity, scale=scale[:, 0:1], bias=scale[:, 1:2]
                )
            normalised[b] = y

        def spread_gain():
            gain_bank = banks.tile([P, 2 * P], F32, name="gain_bank", tag="bank")
            for u in range(2):
                nc.tensor.transpose(
                    gain_bank[:, u * P : (u + 1) * P], gain_rows[:].bitcast(F32)[:, u : 2 * P : 2], identity[:]
                )
            nc.vector.tensor_copy(
                out=gain[:].rearrange("p (g u e) -> p g u e", u=2, e=2),
                in_=gain_bank[:].bitcast(BF16).rearrange("p (u r e) -> p r u e", u=2, e=2)[:, 0:PASSES, :, :],
            )

        def x_transpose(b):
            y = normalised[b]
            grouped = grouped_tiles.tile([P, PASSES * P * PACK], BF16, name="x_grouped", tag="x", align_bytes=64)
            for g in range(PASSES):
                bank = banks.tile([P, PACK * P], F32, name="x_bank", tag="bank")
                for t in range(PACK):
                    column = (g * PACK + t) * P
                    nc.tensor.transpose(bank[:, t * P : (t + 1) * P], y[:, column : column + P], identity[:])
                nc.vector.tensor_tensor(
                    out=grouped[:, g * P * PACK : (g + 1) * P * PACK].rearrange("p (r t) -> p r t", t=PACK),
                    in0=bank[:].rearrange("p (t r) -> p r t", t=PACK),
                    in1=gain[:, g * PACK : (g + 1) * PACK].unsqueeze(1).to_broadcast([P, P, PACK]),
                    op=ALU.mult,
                )
            x_grouped[b] = grouped

        def x_quantise(b):
            columns = slice(b * PASSES * P, (b + 1) * PASSES * P)
            nc.vector.quantize_mx(
                out=x_codes[:, columns].bitcast(FP8X4), scales=x_scales[:, columns], in_=x_grouped[b][:]
            )

        w_grouped = {}

        def w_transpose(run):
            chunk = run // 2
            if run % 2 == 0:
                w_grouped[chunk] = grouped_tiles.tile(
                    [P, PASSES * chunk_width(chunk) * PACK], BF16, name="w_grouped", tag="w", align_bytes=64
                )
            grouped_words = w_grouped[chunk][:].bitcast(F32).rearrange("p (g n u) -> p g n u", g=PASSES, u=2)
            for i in range(RUN_ROW_BLOCKS):
                block = run % 2 * RUN_ROW_BLOCKS + i
                bank = banks.tile([P, PACK * P], F32, name="w_bank", tag="bank")
                for a in range(PACK):
                    first = (chunk_row_block(chunk) + block) * WORDS + a // 2 * 2 * P
                    nc.tensor.transpose(
                        bank[:, a * P : (a + 1) * P], w_words[:, first + a % 2 : first + 2 * P : 2], identity[:]
                    )
                nc.scalar.copy(
                    out=grouped_words[:, :, block * P : (block + 1) * P, :],
                    in_=bank[:].rearrange("p (g u r) -> p g r u", g=PASSES, u=2),
                )

        def completes_chunk(run):
            return 0 <= run < N_RUNS and (run % 2 == 1 or run // 2 == QK_CHUNK)

        def w_quantise(chunk):
            first = chunk * PASSES * CHUNK
            columns = slice(first, first + PASSES * chunk_width(chunk))
            nc.vector.quantize_mx(
                out=w_codes[:, columns].bitcast(FP8X4), scales=w_scales[:, columns], in_=w_grouped[chunk][:]
            )

        def multiply(acc, b, chunk):
            width = chunk_width(chunk)
            for g in range(PASSES):
                rows = slice((b * PASSES + g) * P, (b * PASSES + g + 1) * P)
                first = chunk * PASSES * CHUNK + g * width
                columns = slice(first, first + width)
                nc.tensor.matmul_mx(
                    out=acc,
                    lhsT=x_codes[:, rows].bitcast(FP8X4),
                    lhsT_scale=x_scales[:, rows],
                    rhs=w_codes[:, columns].bitcast(FP8X4),
                    rhs_scale=w_scales[:, columns],
                    start=(g == 0),
                    stop=(g == PASSES - 1),
                )

        def project_qk(b):
            acc = banks.tile([P, QK], F32, name="qk_acc", tag="bank")
            multiply(acc[:], b, QK_CHUNK)
            nc.scalar.copy(out=qk_stage[:, :, b, :], in_=acc[:].rearrange("p (h d) -> p h d", h=2))

        def multiply_pre(b, pair):
            pre = banks.tile([P, CHUNK], F32, name="pre", tag="bank")
            multiply(pre[:], b, 2 * pair + PRE)
            gate = gates.tile([P, CHUNK], F32, name="gate", tag="gate")
            nc.scalar.activation(out=gate[:], in_=pre[:], func=ACT.Gelu)
            return b, pair, gate

        def multiply_lin(product):
            b, pair, gate = product
            lin = banks.tile([P, CHUNK], F32, name="lin", tag="bank")
            multiply(lin[:], b, 2 * pair + LIN)
            return b, pair, gate, lin

        def gate_and_store(product):
            b, pair, gate, lin = product
            geglu = results.tile([P, CHUNK], F32, name="geglu", tag="geglu")
            nc.vector.tensor_tensor(out=geglu[:], in0=lin[:], in1=gate[:], op=ALU.mult)
            nc.sync.dma_start(out=geglu_rows[:, b, pair * CHUNK : (pair + 1) * CHUNK], in_=geglu[:])

        def keep_busy(count):
            idle_bank = banks.tile([P, CHUNK], F32, name="idle_bank", tag="bank")
            for i in range(count):
                nc.tensor.matmul(idle_bank[:], lhsT=filler[:, 0:P], rhs=filler[:], start=True, stop=True)

        nc.vector.memset(gain_rows[:].bitcast(F32), 0.0)
        nc.vector.memset(minus_half[:], -0.5)
        nc.vector.memset(filler[:], 1.0)
        nc.scalar.activation(out=warm[:], in_=minus_half[:], func=ACT.Gelu)
        masks.make_identity(nc, identity[:])

        load_x(0, 1)
        nc.sync.dma_start(out=gain_rows[0:PASSES, :], in_=norm_w.rearrange("(g c) -> g c", g=PASSES))
        for b in range(1, FIRST_BLOCKS):
            load_x(b, 1)
        for chunk in range(QK_CHUNK + 1):
            load_chunk(chunk, 2 if chunk // 2 == 0 else 1)
            if chunk == 2 * 1 + LIN:
                load_x(FIRST_BLOCKS, N_BLOCKS - FIRST_BLOCKS)

        def block_due_at(n):
            if 0 <= n < FIRST_BLOCKS:
                return n
            late = n - FIRST_BLOCKS * STEPS
            if late >= 0 and late % 3 == 0 and late // 3 < N_BLOCKS - FIRST_BLOCKS:
                return FIRST_BLOCKS + late // 3
            return None

        keep_busy(8)
        held = None
        for n in range(-STATISTICS_AHEAD, N_PRODUCTS + 1):
            rnd, step = n // STEPS, n % STEPS
            run = n + RUNS_AHEAD
            if completes_chunk(run - 1):
                w_quantise((run - 1) // 2)
            if 0 <= n + STATISTICS_AHEAD < FIRST_BLOCKS:
                x_statistics(n + STATISTICS_AHEAD)
                x_scale(n + STATISTICS_AHEAD)
                x_normalise(n + STATISTICS_AHEAD)
            if 0 <= n - QK_FROM < N_BLOCKS:
                project_qk(n - QK_FROM)
            if n == QK_FROM + N_BLOCKS:
                nc.sync.dma_start(out=q_rows, in_=qk_stage[:, 0, :, :])
                nc.sync.dma_start(out=k_rows, in_=qk_stage[:, 1, :, :])
            if 0 <= run < N_RUNS:
                w_transpose(run)
            if n + TRANSPOSE_AHEAD == 0:
                spread_gain()
            if block_due_at(n + TRANSPOSE_AHEAD) is not None:
                x_transpose(block_due_at(n + TRANSPOSE_AHEAD))
            if block_due_at(n + QUANTISE_AHEAD) is not None:
                x_quantise(block_due_at(n + QUANTISE_AHEAD))
            product = None if held is None else multiply_lin(held)
            held = None
            if 0 <= n < N_PRODUCTS:
                b, pair = (step, rnd) if rnd < FIRST_BLOCKS else (rnd, step)
                held = multiply_pre(b, pair)
            ready = block_due_at(n + APPLY_AHEAD)
            if ready is not None and ready >= FIRST_BLOCKS:
                x_normalise(ready)
            begun = block_due_at(n + LATE_AHEAD)
            begun = None if begun is None or begun < FIRST_BLOCKS else begun
            if begun is not None:
                x_statistics(begun)
            if product is not None:
                gate_and_store(product)
            if begun is not None:
                x_scale(begun)
